import numpy as np
import ml_dtypes


def mxq(x, axis, fmt="e4m3"):
    dtype, down = {"e4m3": (ml_dtypes.float8_e4m3fn, 7), "e5m2": (ml_dtypes.float8_e5m2, 14)}[fmt]
    v = np.moveaxis(np.asarray(x, np.float32).astype(ml_dtypes.bfloat16).astype(np.float64), axis, -1)
    blocks = v.reshape(v.shape[:-1] + (-1, 32))
    amax = np.abs(blocks).max(-1, keepdims=True)
    byte = np.maximum(np.where(amax > 0, np.frexp(amax)[1] - 1 + 127, 0) - down, 1)
    scale = np.exp2(byte - 127.0)
    codes = (blocks / scale).astype(np.float32).astype(dtype).astype(np.float64)
    return np.moveaxis((codes * scale).reshape(v.shape), -1, axis)


WIDE = False


def mx_kscale(k):
    if not WIDE:
        return np.ones(k)
    levels = np.array([10, -10, 5, -5, 0])
    if k % 512:
        return np.exp2(np.random.permutation(np.resize(levels, k // 32))).repeat(32)
    a = np.empty((k // 512, 16))
    for p in range(k // 512):
        a[p, :8] = np.random.permutation(np.resize(levels, 8))
        for g in range(8):
            far = levels[np.abs(levels - a[p, g]) >= 10]
            a[p, g + 8] = far[np.random.randint(len(far))]
    return np.exp2(a.ravel()).repeat(32)


BF16 = ml_dtypes.bfloat16


def bf(x):
    return np.asarray(x, np.float32).astype(BF16)


def f64(x):
    return np.asarray(x).astype(np.float64)


E2M1 = np.array([0.0, 0.5, 1.0, 1.5, 2.0, 3.0, 4.0, 6.0, -0.0, -0.5, -1.0, -1.5, -2.0, -3.0, -4.0, -6.0])


def pack_weight(w, fmt):
    k, n = w.shape
    w = f64(bf(w)).reshape(k // 32, 32, n)
    amax = np.abs(w).max(1)
    if fmt == "e4m3":
        byte = np.frexp(amax)[1] - 1 + 127 - 7
    else:
        mant, ex = np.frexp(amax / 6.0)
        byte = np.where(mant > 0.5, ex, ex - 1) + 127
    byte = np.clip(np.where(amax > 0, byte, 1), 1, 254)
    scaled = (w * np.exp2(127.0 - byte)[:, None, :]).reshape(k, n).astype(np.float32)
    by_word = np.ascontiguousarray(scaled.reshape(k // 512, 128, 4, n).transpose(0, 1, 3, 2))
    if fmt == "e4m3":
        words = by_word.astype(ml_dtypes.float8_e4m3fn).view(np.uint8)
    else:
        c = by_word.astype(ml_dtypes.float4_e2m1fn).view(np.uint8) & 0xF
        words = c[..., 0::2] | (c[..., 1::2] << 4)
    return np.ascontiguousarray(words), np.ascontiguousarray(byte.astype(np.uint8).reshape(k // 512, 16, n))


def unpack_weight(words, scales, fmt):
    g, p, n, _ = words.shape
    if fmt == "e4m3":
        vals = np.ascontiguousarray(words).view(ml_dtypes.float8_e4m3fn).astype(np.float64)
    else:
        nib = np.empty((g, p, n, 4), np.uint8)
        nib[..., 0::2] = words & 0xF
        nib[..., 1::2] = words >> 4
        vals = E2M1[nib]
    vals = vals * np.repeat(np.exp2(scales.astype(np.float64) - 127.0), 8, axis=1)[..., None]
    return vals.transpose(0, 1, 3, 2).reshape(g * 512, n)
def pack4(w):
    words, scales = pack_weight(w, "e2m1")
    return words.reshape(words.shape[0], 128, -1), scales


def unpack4(words, scales):
    return unpack_weight(words.reshape(words.shape[0], 128, -1, 2), scales, "e2m1")


B, D_IN, HID, OUT = 8192, 512, 512, 128


def draw0():
    s, t = mx_kscale(D_IN), mx_kscale(HID)
    u = np.concatenate([s, t])
    x = bf(np.random.standard_normal((B, D_IN)) * s)
    W1 = np.random.standard_normal((HID, D_IN)) / np.sqrt(D_IN) / s[None, :] * t[:, None]
    W1_words, W1_scales = pack4(W1.T)
    b1 = bf(np.random.standard_normal(HID) * 0.3 * t)
    W2 = np.random.standard_normal((OUT, D_IN + HID)) / np.sqrt(D_IN + HID) / u[None, :]
    W2_words, W2_scales = pack4(W2.T)
    b2 = bf(np.random.standard_normal(OUT) * 0.3)
    return {"x": x,
            "W1_words": W1_words,
            "W1_scales": W1_scales,
            "b1": b1,
            "W2_words": W2_words,
            "W2_scales": W2_scales,
            "b2": b2}


def core(x, W1_words, W1_scales, b1, W2_words, W2_scales, b2):
    xq = mxq(f64(x), 1, "e4m3")
    h1 = np.maximum((xq @ unpack4(W1_words, W1_scales)) + f64(b1), 0.0)
    concat = np.concatenate([xq, mxq(h1, 1, "e4m3")], axis=1)
    return (concat @ unpack4(W2_words, W2_scales)) + f64(b2)


def e4m3fn_bytes(y):
    return np.clip(np.asarray(y, np.float64), -448.0, 448.0).astype(np.float32).astype(ml_dtypes.float8_e4m3fn).view(np.uint8)


def e4m3fn_values(b):
    return np.asarray(b, np.uint8).view(ml_dtypes.float8_e4m3fn).astype(np.float64)


def setup_inputs():
    d = draw0()
    x0 = np.asarray(d['x']).astype(np.float64)
    s = (np.max(np.abs(x0), axis=(0,), keepdims=True) / 448.0).astype(np.float32)
    out = {}
    for k, v in d.items():
        if k == 'x':
            out['x_bytes'] = e4m3fn_bytes(x0 / s.astype(np.float64))
            out['x_scale'] = s
        else:
            out[k] = v
    return out


def reference(x_bytes, x_scale, W1_words, W1_scales, b1, W2_words, W2_scales, b2):
    return core(e4m3fn_values(x_bytes) * x_scale.astype(np.float64), W1_words, W1_scales, b1, W2_words, W2_scales, b2)

@@ -1,0 +1,252 @@
+from contextlib import ExitStack
+
+import concourse.mybir as mybir
+from concourse.masks import make_identity
+
+ROWS, D_IN, HID, OUT = 8192, 512, 512, 128
+FLOPS = 2 * ROWS * D_IN * HID + 2 * ROWS * (D_IN + HID) * OUT
+
+F32 = mybir.dt.float32
+BF16 = mybir.dt.bfloat16
+U32 = mybir.dt.uint32
+I32 = mybir.dt.int32
+U8 = mybir.dt.uint8
+FP8 = mybir.dt.float8_e4m3fn
+FP8X4 = mybir.dt.float8_e4m3fn_x4
+FP4X4 = mybir.dt.float4_e2m1fn_x4
+ADD = mybir.AluOpType.add
+MULT = mybir.AluOpType.mult
+RELU = mybir.ActivationFunctionType.Relu
+
+P = 128
+PACK = 4
+MAX_TILES = 4
+UNITS = [4] * 15 + [2, 2]
+N_UNITS = len(UNITS)
+STARTS = [P * sum(UNITS[:c]) for c in range(N_UNITS)]
+assert P * sum(UNITS) == ROWS
+
+
+def tile_dpn_t_w4_kernel(tc, x_bytes, x_scale, W1_words, W1_scales, b1, W2_words, W2_scales, b2, out):
+    nc = tc.nc
+
+    with ExitStack() as ctx:
+        keep = ctx.enter_context(tc.tile_pool(name="keep", bufs=1))
+        work = ctx.enter_context(tc.tile_pool(name="work", bufs=3))
+        psum = ctx.enter_context(tc.psum_pool(name="psum", bufs=1))
+
+        ident = keep.tile([P, P], F32, name="ident")
+        scale_row = keep.tile([P, 2 * D_IN], F32, name="scale_row")
+        w1_raw = keep.tile([P, HID * 2], U8, name="w1_raw", align_bytes=64)
+        w1 = keep.tile([P, HID * 2], U8, name="w1", align_bytes=64)
+        w1s_raw = keep.tile([P, HID], U8, name="w1s_raw", align_bytes=64)
+        w1s = keep.tile([P, HID], U8, name="w1s", align_bytes=64)
+        w2 = keep.tile([P, 2, OUT * 2], U8, name="w2", align_bytes=64)
+        w2s = keep.tile([P, 2, OUT], U8, name="w2s", align_bytes=64)
+        b1_col = keep.tile([P, PACK], BF16, name="b1_col")
+        b1_f32 = keep.tile([P, PACK], F32, name="b1_f32")
+        b2_row = keep.tile([P, OUT], BF16, name="b2_row")
+        warm = keep.tile([P, 1], F32, name="warm")
+
+        x8 = {}
+
+        def load(c):
+            tiles = UNITS[c]
+            x8[c] = work.tile([P, MAX_TILES * D_IN], U8, name="x8", bufs=N_UNITS, align_bytes=64)
+            nc.sync.dma_start(
+                out=x8[c][:, : tiles * D_IN],
+                in_=x_bytes[STARTS[c] : STARTS[c] + P * tiles, :].rearrange("(p j) k -> p (j k)", j=tiles),
+            )
+
+        nc.scalar.dma_start(out=scale_row[:, :D_IN], in_=x_scale.rearrange("o k -> (o k)").partition_broadcast(P))
+        load(0)
+        nc.vector.memset(warm[:], 0.0)
+        nc.vector.memset(w1s_raw[:].bitcast(U32), 0)
+        nc.vector.memset(w2s[:].rearrange("p g n -> p (g n)").bitcast(U32), 0)
+        nc.scalar.activation(out=warm[:], in_=warm[:], func=RELU)
+        nc.scalar.copy(out=scale_row[:, D_IN:], in_=scale_row[:, :D_IN])
+        make_identity(nc, ident[:])
+        nc.sync.dma_start(out=w1_raw[:], in_=W1_words[0])
+        for q in range(4):
+            nc.sync.dma_start(
+                out=w1s_raw[32 * q : 32 * q + 4, :].bitcast(I32), in_=W1_scales[0, 4 * q : 4 * q + 4, :].bitcast(I32)
+            )
+        nc.scalar.dma_start(out=b1_col[:], in_=b1.rearrange("(p t) -> p t", t=PACK))
+        load(1)
+        load(2)
+        nc.sync.dma_start(out=w2[:], in_=W2_words.rearrange("g p n -> p g n"))
+        for q in range(4):
+            nc.sync.dma_start(
+                out=w2s[32 * q : 32 * q + 4, :, :].bitcast(I32),
+                in_=W2_scales.bitcast(I32)[:, 4 * q : 4 * q + 4, :].rearrange("g q n -> q g n"),
+            )
+        load(3)
+        nc.sync.dma_start(out=b2_row[:], in_=b2.partition_broadcast(P))
+        for c in range(4, N_UNITS):
+            load(c)
+
+        def permute_weights():
+            nc.vector.tensor_copy(
+                out=w1[:].rearrange("p (t m b) -> p t m b", t=PACK, b=2),
+                in_=w1_raw[:].rearrange("p (m t b) -> p t m b", t=PACK, b=2),
+            )
+            nc.vector.tensor_copy(
+                out=w1s[:].rearrange("p (t m) -> p t m", t=PACK),
+                in_=w1s_raw[:].rearrange("p (m t) -> p t m", t=PACK),
+            )
+            nc.vector.tensor_copy(out=b1_f32[:], in_=b1_col[:])
+
+        xb, xt, xg, xq, xs = {}, {}, {}, {}, {}
+        h, hs, hg, hq, hsc = {}, {}, {}, {}, {}
+        acc, ob = {}, {}
+
+        def live(c, half=0):
+            return 0 <= c < N_UNITS and 2 * half < UNITS[c]
+
+        def scale_x(c, half):
+            if not live(c, half):
+                return
+            if half == 0:
+                xb[c] = work.tile([P, MAX_TILES * D_IN], BF16, name="xb", align_bytes=64)
+            cols = slice(2 * half * D_IN, 2 * (half + 1) * D_IN)
+            nc.vector.tensor_tensor(out=xb[c][:, cols], in0=x8[c][:, cols].bitcast(FP8), in1=scale_row[:], op=MULT)
+
+        def transpose_x(c, half):
+            if not live(c, half):
+                return
+            words = xb[c][:].bitcast(F32)
+            xt[c, half] = psum.tile([P, 4, P], F32, name="xt", bufs=2)
+            for j in range(2):
+                for u in range(2):
+                    w0 = (2 * half + j) * (D_IN // 2)
+                    nc.tensor.transpose(
+                        xt[c, half][:, 2 * j + u, :], words[:, w0 + u : w0 + D_IN // 2 : 2], ident[:]
+                    )
+
+        def gather_x(c, half):
+            if not live(c, half):
+                return
+            if half == 0:
+                xg[c] = work.tile([P, MAX_TILES * D_IN], BF16, name="xg", align_bytes=64)
+            dst = xg[c][:].bitcast(F32)[:, 512 * half : 512 * (half + 1)]
+            nc.scalar.copy(
+                out=dst.rearrange("p (j n u) -> p j n u", j=2, u=2),
+                in_=xt[c, half][:].rearrange("p (j u) n -> p j n u", u=2),
+            )
+
+        def quantize_x(c):
+            if not live(c):
+                return
+            n = P * UNITS[c]
+            xq[c] = work.tile([P, MAX_TILES * P], U32, name="xq", bufs=5, align_bytes=64)
+            xs[c] = work.tile([P, MAX_TILES * P], U8, name="xs", bufs=5, align_bytes=64)
+            nc.vector.quantize_mx(
+                out=xq[c][:, :n].bitcast(FP8X4), scales=xs[c][:, :n], in_=xg[c][:, : PACK * n]
+            )
+
+        def layer1(c, t):
+            if not live(c):
+                return
+            n = P * UNITS[c]
+            h[c, t] = psum.tile([P, MAX_TILES * P], F32, name="h%d" % t)
+            nc.tensor.matmul_mx(
+                out=h[c, t][:, :n],
+                lhsT=w1[:, 2 * P * t : 2 * P * (t + 1)].bitcast(FP4X4),
+                lhsT_scale=w1s[:, P * t : P * (t + 1)],
+                rhs=xq[c][:, :n].bitcast(FP8X4),
+                rhs_scale=xs[c][:, :n],
+                start=True,
+                stop=True,
+            )
+
+        def relu(c, t):
+            if not live(c):
+                return
+            n = P * UNITS[c]
+            if c not in hs:
+                hs[c] = work.tile([P, 2, MAX_TILES * P, 2], BF16, name="hs", align_bytes=64)
+            dst = hs[c][:, t // 2, :n, t % 2]
+            nc.scalar.activation(out=dst, in_=h[c, t][:, :n], func=RELU, bias=b1_f32[:, t : t + 1])
+
+        def interleave_h(c):
+            if not live(c):
+                return
+            n = P * UNITS[c]
+            hg[c] = work.tile([P, MAX_TILES * D_IN], BF16, name="hg", align_bytes=64)
+            words = hs[c][:].rearrange("p a n e -> p (a n e)").bitcast(F32).rearrange("p (a n) -> p n a", a=2)
+            nc.vector.tensor_copy(
+                out=hg[c][:, : PACK * n].bitcast(F32).rearrange("p (n a) -> p n a", a=2), in_=words[:, :n, :]
+            )
+
+        def quantize_h(c):
+            if not live(c):
+                return
+            n = P * UNITS[c]
+            hq[c] = work.tile([P, MAX_TILES * P], U32, name="hq", align_bytes=64)
+            hsc[c] = work.tile([P, MAX_TILES * P], U8, name="hsc", align_bytes=64)
+            nc.vector.quantize_mx(
+                out=hq[c][:, :n].bitcast(FP8X4), scales=hsc[c][:, :n], in_=hg[c][:, : PACK * n]
+            )
+
+        def layer2(c):
+            if not live(c):
+                return
+            acc[c] = psum.tile([P, MAX_TILES, OUT], F32, name="acc", bufs=2)
+            for j in range(UNITS[c]):
+                cols = slice(P * j, P * (j + 1))
+                for g, codes, scales in ((0, xq[c], xs[c]), (1, hq[c], hsc[c])):
+                    nc.tensor.matmul_mx(
+                        out=acc[c][:, j, :],
+                        lhsT=codes[:, cols].bitcast(FP8X4),
+                        lhsT_scale=scales[:, cols],
+                        rhs=w2[:, g, :].bitcast(FP4X4),
+                        rhs_scale=w2s[:, g, :],
+                        start=(g == 0),
+                        stop=(g == 1),
+                    )
+
+        def add_b2(c):
+            if not live(c):
+                return
+            tiles = UNITS[c]
+            ob[c] = work.tile([P, MAX_TILES, OUT], F32, name="ob")
+            nc.vector.tensor_tensor(
+                out=ob[c][:, :tiles, :],
+                in0=acc[c][:, :tiles, :],
+                in1=b2_row[:].unsqueeze(1).to_broadcast([P, tiles, OUT]),
+                op=ADD,
+            )
+
+        def store(c):
+            if not live(c):
+                return
+            tiles = UNITS[c]
+            nc.sync.dma_start(
+                out=out[STARTS[c] : STARTS[c] + P * tiles, :].rearrange("(p j) o -> p (j o)", j=tiles),
+                in_=ob[c][:, :tiles, :].rearrange("p j o -> p (j o)"),
+            )
+
+        with tc.manual_schedule():
+            for s in range(-5, N_UNITS):
+                relu(s + 1, 3)
+                layer1(s + 2, 0)
+                gather_x(s + 3, 0)
+                scale_x(s + 4, 1)
+                if s == -4:
+                    permute_weights()
+                layer1(s + 2, 1)
+                interleave_h(s + 1)
+                layer2(s)
+                layer1(s + 2, 2)
+                gather_x(s + 3, 1)
+                layer1(s + 2, 3)
+                quantize_x(s + 3)
+                transpose_x(s + 4, 0)
+                transpose_x(s + 4, 1)
+                scale_x(s + 5, 0)
+                relu(s + 2, 0)
+                quantize_h(s + 1)
+                relu(s + 2, 1)
+                relu(s + 2, 2)
+                add_b2(s)
+                store(s)

@@ -36,7 +36,7 @@ def tile_dpn_t_w4_kernel(tc, x_bytes, x_scale, W1_words, W1_scales, b1, W2_words
         psum = ctx.enter_context(tc.psum_pool(name="psum", bufs=1))
 
         ident = keep.tile([P, P], F32, name="ident")
-        scale_row = keep.tile([P, 2 * D_IN], F32, name="scale_row")
+        scale_row = keep.tile([P, MAX_TILES * D_IN], F32, name="scale_row")
         w1_raw = keep.tile([P, HID * 2], U8, name="w1_raw", align_bytes=64)
         w1 = keep.tile([P, HID * 2], U8, name="w1", align_bytes=64)
         w1s_raw = keep.tile([P, HID], U8, name="w1s_raw", align_bytes=64)
@@ -44,34 +44,37 @@ def tile_dpn_t_w4_kernel(tc, x_bytes, x_scale, W1_words, W1_scales, b1, W2_words
         w2 = keep.tile([P, 2, OUT * 2], U8, name="w2", align_bytes=64)
         w2s = keep.tile([P, 2, OUT], U8, name="w2s", align_bytes=64)
         b1_col = keep.tile([P, PACK], BF16, name="b1_col")
-        b1_f32 = keep.tile([P, PACK], F32, name="b1_f32")
         b2_row = keep.tile([P, OUT], BF16, name="b2_row")
         warm = keep.tile([P, 1], F32, name="warm")
 
         x8 = {}
 
-        def load(c):
+        def load(c, lo=0, hi=MAX_TILES):
             tiles = UNITS[c]
-            x8[c] = work.tile([P, MAX_TILES * D_IN], U8, name="x8", bufs=N_UNITS, align_bytes=64)
-            nc.sync.dma_start(
-                out=x8[c][:, : tiles * D_IN],
-                in_=x_bytes[STARTS[c] : STARTS[c] + P * tiles, :].rearrange("(p j) k -> p (j k)", j=tiles),
-            )
+            if lo == 0:
+                x8[c] = work.tile([P, MAX_TILES * D_IN], U8, name="x8", bufs=N_UNITS, align_bytes=64)
+            cols = slice(D_IN * lo, D_IN * min(hi, tiles))
+            src = x_bytes[STARTS[c] : STARTS[c] + P * tiles, :].rearrange("(p j) k -> p (j k)", j=tiles)
+            nc.sync.dma_start(out=x8[c][:, cols], in_=src[:, cols])
 
-        nc.scalar.dma_start(out=scale_row[:, :D_IN], in_=x_scale.rearrange("o k -> (o k)").partition_broadcast(P))
-        load(0)
-        nc.vector.memset(warm[:], 0.0)
         nc.vector.memset(w1s_raw[:].bitcast(U32), 0)
         nc.vector.memset(w2s[:].rearrange("p g n -> p (g n)").bitcast(U32), 0)
-        nc.scalar.activation(out=warm[:], in_=warm[:], func=RELU)
-        nc.scalar.copy(out=scale_row[:, D_IN:], in_=scale_row[:, :D_IN])
-        make_identity(nc, ident[:])
+        nc.vector.memset(warm[:], 0.0)
+        nc.scalar.dma_start(out=scale_row[:, :D_IN], in_=x_scale.rearrange("o k -> (o k)").partition_broadcast(P))
+        load(0, 0, 2)
         nc.sync.dma_start(out=w1_raw[:], in_=W1_words[0])
         for q in range(4):
             nc.sync.dma_start(
                 out=w1s_raw[32 * q : 32 * q + 4, :].bitcast(I32), in_=W1_scales[0, 4 * q : 4 * q + 4, :].bitcast(I32)
             )
+        load(0, 2, 4)
         nc.scalar.dma_start(out=b1_col[:], in_=b1.rearrange("(p t) -> p t", t=PACK))
+        nc.scalar.activation(out=warm[:], in_=warm[:], func=RELU)
+        nc.scalar.copy(
+            out=scale_row[:, D_IN:].rearrange("p (j k) -> p j k", k=D_IN),
+            in_=scale_row[:, :D_IN].unsqueeze(1).to_broadcast([P, MAX_TILES - 1, D_IN]),
+        )
+        make_identity(nc, ident[:])
         load(1)
         load(2)
         nc.sync.dma_start(out=w2[:], in_=W2_words.rearrange("g p n -> p g n"))
@@ -80,9 +83,8 @@ def tile_dpn_t_w4_kernel(tc, x_bytes, x_scale, W1_words, W1_scales, b1, W2_words
                 out=w2s[32 * q : 32 * q + 4, :, :].bitcast(I32),
                 in_=W2_scales.bitcast(I32)[:, 4 * q : 4 * q + 4, :].rearrange("g q n -> q g n"),
             )
-        load(3)
         nc.sync.dma_start(out=b2_row[:], in_=b2.partition_broadcast(P))
-        for c in range(4, N_UNITS):
+        for c in range(3, N_UNITS):
             load(c)
 
         def permute_weights():
@@ -94,7 +96,6 @@ def tile_dpn_t_w4_kernel(tc, x_bytes, x_scale, W1_words, W1_scales, b1, W2_words
                 out=w1s[:].rearrange("p (t m) -> p t m", t=PACK),
                 in_=w1s_raw[:].rearrange("p (m t) -> p t m", t=PACK),
             )
-            nc.vector.tensor_copy(out=b1_f32[:], in_=b1_col[:])
 
         xb, xt, xg, xq, xs = {}, {}, {}, {}, {}
         h, hs, hg, hq, hsc = {}, {}, {}, {}, {}
@@ -103,13 +104,18 @@ def tile_dpn_t_w4_kernel(tc, x_bytes, x_scale, W1_words, W1_scales, b1, W2_words
         def live(c, half=0):
             return 0 <= c < N_UNITS and 2 * half < UNITS[c]
 
-        def scale_x(c, half):
-            if not live(c, half):
+        def scale_x(c, lo=0, hi=MAX_TILES):
+            if not live(c):
                 return
-            if half == 0:
+            if lo == 0:
                 xb[c] = work.tile([P, MAX_TILES * D_IN], BF16, name="xb", align_bytes=64)
-            cols = slice(2 * half * D_IN, 2 * (half + 1) * D_IN)
-            nc.vector.tensor_tensor(out=xb[c][:, cols], in0=x8[c][:, cols].bitcast(FP8), in1=scale_row[:], op=MULT)
+            cols = slice(D_IN * lo, D_IN * min(hi, UNITS[c]))
+            nc.vector.tensor_tensor(
+                out=xb[c][:, cols],
+                in0=x8[c][:, cols].bitcast(FP8),
+                in1=scale_row[:, : cols.stop - cols.start],
+                op=MULT,
+            )
 
         def transpose_x(c, half):
             if not live(c, half):
@@ -129,7 +135,8 @@ def tile_dpn_t_w4_kernel(tc, x_bytes, x_scale, W1_words, W1_scales, b1, W2_words
             if half == 0:
                 xg[c] = work.tile([P, MAX_TILES * D_IN], BF16, name="xg", align_bytes=64)
             dst = xg[c][:].bitcast(F32)[:, 512 * half : 512 * (half + 1)]
-            nc.scalar.copy(
+            copy = nc.scalar.copy if c < N_UNITS - 2 else nc.vector.tensor_copy
+            copy(
                 out=dst.rearrange("p (j n u) -> p j n u", j=2, u=2),
                 in_=xt[c, half][:].rearrange("p (j u) n -> p j n u", u=2),
             )
@@ -166,7 +173,7 @@ def tile_dpn_t_w4_kernel(tc, x_bytes, x_scale, W1_words, W1_scales, b1, W2_words
             if c not in hs:
                 hs[c] = work.tile([P, 2, MAX_TILES * P, 2], BF16, name="hs", align_bytes=64)
             dst = hs[c][:, t // 2, :n, t % 2]
-            nc.scalar.activation(out=dst, in_=h[c, t][:, :n], func=RELU, bias=b1_f32[:, t : t + 1])
+            nc.scalar.activation(out=dst, in_=h[c, t][:, :n], func=RELU, bias=b1_col[:, t : t + 1])
 
         def interleave_h(c):
             if not live(c):
@@ -227,26 +234,46 @@ def tile_dpn_t_w4_kernel(tc, x_bytes, x_scale, W1_words, W1_scales, b1, W2_words
             )
 
         with tc.manual_schedule():
-            for s in range(-5, N_UNITS):
-                relu(s + 1, 3)
-                layer1(s + 2, 0)
+            scale_x(0, 0, 1)
+            scale_x(0, 1, 2)
+            permute_weights()
+            scale_x(0, 2, 3)
+            scale_x(0, 3, 4)
+            transpose_x(0, 0)
+            transpose_x(0, 1)
+            gather_x(0, 0)
+            gather_x(0, 1)
+            scale_x(1, 0, 2)
+            quantize_x(0)
+            for t in range(PACK):
+                layer1(0, t)
+            scale_x(1, 2, 4)
+            transpose_x(1, 0)
+            transpose_x(1, 1)
+            relu(0, 0)
+            relu(0, 1)
+            gather_x(1, 0)
+            gather_x(1, 1)
+            relu(0, 2)
+            relu(0, 3)
+            scale_x(2)
+            quantize_x(1)
+            transpose_x(2, 0)
+            transpose_x(2, 1)
+            scale_x(3)
+            for s in range(-1, N_UNITS):
+                for t in range(PACK):
+                    layer1(s + 2, t)
                 gather_x(s + 3, 0)
-                scale_x(s + 4, 1)
-                if s == -4:
-                    permute_weights()
-                layer1(s + 2, 1)
-                interleave_h(s + 1)
-                layer2(s)
-                layer1(s + 2, 2)
                 gather_x(s + 3, 1)
-                layer1(s + 2, 3)
-                quantize_x(s + 3)
                 transpose_x(s + 4, 0)
                 transpose_x(s + 4, 1)
-                scale_x(s + 5, 0)
-                relu(s + 2, 0)
+                interleave_h(s + 1)
+                quantize_x(s + 3)
+                scale_x(s + 5)
+                layer2(s)
+                for t in range(PACK):
+                    relu(s + 2, t)
                 quantize_h(s + 1)
-                relu(s + 2, 1)
-                relu(s + 2, 2)
                 add_b2(s)
                 store(s)

@@ -23,6 +23,8 @@ PACK = 4
 MAX_TILES = 4
 UNITS = [4] * 15 + [2, 2]
 N_UNITS = len(UNITS)
+VECTOR_WIDENS = {(4, 0), (9, 0)}
+VECTOR_PARTS = {N_UNITS - 1: 2, N_UNITS - 2: 2, N_UNITS - 3: 3, N_UNITS - 4: 2, N_UNITS - 5: 1}
 STARTS = [P * sum(UNITS[:c]) for c in range(N_UNITS)]
 assert P * sum(UNITS) == ROWS
 
@@ -36,7 +38,7 @@ def tile_dpn_t_w4_kernel(tc, x_bytes, x_scale, W1_words, W1_scales, b1, W2_words
         psum = ctx.enter_context(tc.psum_pool(name="psum", bufs=1))
 
         ident = keep.tile([P, P], F32, name="ident")
-        scale_row = keep.tile([P, MAX_TILES * D_IN], F32, name="scale_row")
+        x_scales = keep.tile([P, PACK], F32, name="x_scales")
         w1_raw = keep.tile([P, HID * 2], U8, name="w1_raw", align_bytes=64)
         w1 = keep.tile([P, HID * 2], U8, name="w1", align_bytes=64)
         w1s_raw = keep.tile([P, HID], U8, name="w1s_raw", align_bytes=64)
@@ -60,7 +62,7 @@ def tile_dpn_t_w4_kernel(tc, x_bytes, x_scale, W1_words, W1_scales, b1, W2_words
         nc.vector.memset(w1s_raw[:].bitcast(U32), 0)
         nc.vector.memset(w2s[:].rearrange("p g n -> p (g n)").bitcast(U32), 0)
         nc.vector.memset(warm[:], 0.0)
-        nc.scalar.dma_start(out=scale_row[:, :D_IN], in_=x_scale.rearrange("o k -> (o k)").partition_broadcast(P))
+        nc.scalar.dma_start(out=x_scales[:], in_=x_scale.rearrange("o (p t) -> p (o t)", t=PACK))
         load(0, 0, 2)
         nc.sync.dma_start(out=w1_raw[:], in_=W1_words[0])
         for q in range(4):
@@ -70,10 +72,6 @@ def tile_dpn_t_w4_kernel(tc, x_bytes, x_scale, W1_words, W1_scales, b1, W2_words
         load(0, 2, 4)
         nc.scalar.dma_start(out=b1_col[:], in_=b1.rearrange("(p t) -> p t", t=PACK))
         nc.scalar.activation(out=warm[:], in_=warm[:], func=RELU)
-        nc.scalar.copy(
-            out=scale_row[:, D_IN:].rearrange("p (j k) -> p j k", k=D_IN),
-            in_=scale_row[:, :D_IN].unsqueeze(1).to_broadcast([P, MAX_TILES - 1, D_IN]),
-        )
         make_identity(nc, ident[:])
         load(1)
         load(2)
@@ -104,41 +102,38 @@ def tile_dpn_t_w4_kernel(tc, x_bytes, x_scale, W1_words, W1_scales, b1, W2_words
         def live(c, half=0):
             return 0 <= c < N_UNITS and 2 * half < UNITS[c]
 
-        def scale_x(c, lo=0, hi=MAX_TILES):
+        def widen_x(c, lo=0, hi=MAX_TILES):
             if not live(c):
                 return
             if lo == 0:
-                xb[c] = work.tile([P, MAX_TILES * D_IN], BF16, name="xb", align_bytes=64)
+                xb[c] = work.tile([P, MAX_TILES * D_IN], BF16, name="xb", bufs=4, align_bytes=64)
             cols = slice(D_IN * lo, D_IN * min(hi, UNITS[c]))
-            nc.vector.tensor_tensor(
-                out=xb[c][:, cols],
-                in0=x8[c][:, cols].bitcast(FP8),
-                in1=scale_row[:, : cols.stop - cols.start],
-                op=MULT,
-            )
+            copy = nc.vector.tensor_copy if (c, lo) in VECTOR_WIDENS else nc.scalar.copy
+            copy(out=xb[c][:, cols], in_=x8[c][:, cols].bitcast(FP8))
 
         def transpose_x(c, half):
             if not live(c, half):
                 return
             words = xb[c][:].bitcast(F32)
-            xt[c, half] = psum.tile([P, 4, P], F32, name="xt", bufs=2)
+            xt[c, half] = psum.tile([P, 2, 2, P], F32, name="xt", bufs=2)
             for j in range(2):
+                w0 = (2 * half + j) * (D_IN // 2)
                 for u in range(2):
-                    w0 = (2 * half + j) * (D_IN // 2)
-                    nc.tensor.transpose(
-                        xt[c, half][:, 2 * j + u, :], words[:, w0 + u : w0 + D_IN // 2 : 2], ident[:]
-                    )
+                    nc.tensor.transpose(xt[c, half][:, u, j, :], words[:, w0 + u : w0 + D_IN // 2 : 2], ident[:])
 
-        def gather_x(c, half):
+        def scale_x(c, half):
             if not live(c, half):
                 return
             if half == 0:
                 xg[c] = work.tile([P, MAX_TILES * D_IN], BF16, name="xg", align_bytes=64)
-            dst = xg[c][:].bitcast(F32)[:, 512 * half : 512 * (half + 1)]
-            copy = nc.scalar.copy if c < N_UNITS - 2 else nc.vector.tensor_copy
-            copy(
-                out=dst.rearrange("p (j n u) -> p j n u", j=2, u=2),
-                in_=xt[c, half][:].rearrange("p (j u) n -> p j n u", u=2),
+            nc.vector.tensor_tensor(
+                out=xg[c][:, 2 * D_IN * half : 2 * D_IN * (half + 1)].rearrange("p (n u e) -> p n u e", u=2, e=2),
+                in0=xt[c, half][:]
+                .rearrange("p u j n -> p (u j n)")
+                .bitcast(BF16)
+                .rearrange("p (u n e) -> p n u e", u=2, e=2),
+                in1=x_scales[:].rearrange("p (u e) -> p u e", e=2).unsqueeze(1).to_broadcast([P, 2 * P, 2, 2]),
+                op=MULT,
             )
 
         def quantize_x(c):
@@ -171,19 +166,26 @@ def tile_dpn_t_w4_kernel(tc, x_bytes, x_scale, W1_words, W1_scales, b1, W2_words
                 return
             n = P * UNITS[c]
             if c not in hs:
-                hs[c] = work.tile([P, 2, MAX_TILES * P, 2], BF16, name="hs", align_bytes=64)
-            dst = hs[c][:, t // 2, :n, t % 2]
+                hs[c] = work.tile([P, PACK, MAX_TILES * P], BF16, name="hs", align_bytes=64)
+            dst = hs[c][:, t, :n]
             nc.scalar.activation(out=dst, in_=h[c, t][:, :n], func=RELU, bias=b1_col[:, t : t + 1])
 
-        def interleave_h(c):
+        def interleave_h(c, on_vector=False):
             if not live(c):
                 return
-            n = P * UNITS[c]
-            hg[c] = work.tile([P, MAX_TILES * D_IN], BF16, name="hg", align_bytes=64)
-            words = hs[c][:].rearrange("p a n e -> p (a n e)").bitcast(F32).rearrange("p (a n) -> p n a", a=2)
-            nc.vector.tensor_copy(
-                out=hg[c][:, : PACK * n].bitcast(F32).rearrange("p (n a) -> p n a", a=2), in_=words[:, :n, :]
-            )
+            if c not in hg:
+                hg[c] = work.tile([P, MAX_TILES * P, PACK], BF16, name="hg", align_bytes=64)
+            for j in range(UNITS[c]):
+                if on_vector != (j < VECTOR_PARTS.get(c, 0)):
+                    continue
+                rows = slice(P * j, P * (j + 1))
+                src = hs[c][:, :, rows].rearrange("p t n -> p n t")
+                if on_vector:
+                    nc.vector.tensor_copy(out=hg[c][:, rows, :], in_=src)
+                else:
+                    nc.gpsimd.tensor_scalar(
+                        out=hg[c][:, rows, :], in0=src, scalar1=1.0, scalar2=0.0, op0=MULT, op1=ADD
+                    )
 
         def quantize_h(c):
             if not live(c):
@@ -192,7 +194,7 @@ def tile_dpn_t_w4_kernel(tc, x_bytes, x_scale, W1_words, W1_scales, b1, W2_words
             hq[c] = work.tile([P, MAX_TILES * P], U32, name="hq", align_bytes=64)
             hsc[c] = work.tile([P, MAX_TILES * P], U8, name="hsc", align_bytes=64)
             nc.vector.quantize_mx(
-                out=hq[c][:, :n].bitcast(FP8X4), scales=hsc[c][:, :n], in_=hg[c][:, : PACK * n]
+                out=hq[c][:, :n].bitcast(FP8X4), scales=hsc[c][:, :n], in_=hg[c][:, :n, :].rearrange("p n t -> p (n t)")
             )
 
         def layer2(c):
@@ -234,46 +236,27 @@ def tile_dpn_t_w4_kernel(tc, x_bytes, x_scale, W1_words, W1_scales, b1, W2_words
             )
 
         with tc.manual_schedule():
-            scale_x(0, 0, 1)
-            scale_x(0, 1, 2)
+            widen_x(0, 0, 2)
             permute_weights()
-            scale_x(0, 2, 3)
-            scale_x(0, 3, 4)
-            transpose_x(0, 0)
-            transpose_x(0, 1)
-            gather_x(0, 0)
-            gather_x(0, 1)
-            scale_x(1, 0, 2)
-            quantize_x(0)
-            for t in range(PACK):
-                layer1(0, t)
-            scale_x(1, 2, 4)
-            transpose_x(1, 0)
-            transpose_x(1, 1)
-            relu(0, 0)
-            relu(0, 1)
-            gather_x(1, 0)
-            gather_x(1, 1)
-            relu(0, 2)
-            relu(0, 3)
-            scale_x(2)
-            quantize_x(1)
-            transpose_x(2, 0)
-            transpose_x(2, 1)
-            scale_x(3)
-            for s in range(-1, N_UNITS):
-                for t in range(PACK):
-                    layer1(s + 2, t)
-                gather_x(s + 3, 0)
-                gather_x(s + 3, 1)
-                transpose_x(s + 4, 0)
-                transpose_x(s + 4, 1)
-                interleave_h(s + 1)
-                quantize_x(s + 3)
-                scale_x(s + 5)
-                layer2(s)
+            widen_x(0, 2, 4)
+            for s in range(-5, N_UNITS):
                 for t in range(PACK):
                     relu(s + 2, t)
-                quantize_h(s + 1)
+                widen_x(s + 6)
+                if s == -5:
+                    transpose_x(0, 0)
+                    transpose_x(0, 1)
+                quantize_h(s)
+                interleave_h(s + 1)
+                layer2(s)
+                scale_x(s + 4, 0)
+                scale_x(s + 4, 1)
+                for t in range(PACK):
+                    layer1(s + 3, t)
+                interleave_h(s + 1, on_vector=True)
                 add_b2(s)
+                quantize_x(s + 4)
+                if s > -5:
+                    transpose_x(s + 5, 0)
+                    transpose_x(s + 5, 1)
                 store(s)

from contextlib import ExitStack

import concourse.mybir as mybir
from concourse.masks import make_identity

ROWS, D_IN, HID, OUT = 8192, 512, 512, 128
FLOPS = 2 * ROWS * D_IN * HID + 2 * ROWS * (D_IN + HID) * OUT

F32 = mybir.dt.float32
BF16 = mybir.dt.bfloat16
U32 = mybir.dt.uint32
I32 = mybir.dt.int32
U8 = mybir.dt.uint8
FP8 = mybir.dt.float8_e4m3fn
FP8X4 = mybir.dt.float8_e4m3fn_x4
FP4X4 = mybir.dt.float4_e2m1fn_x4
ADD = mybir.AluOpType.add
MULT = mybir.AluOpType.mult
RELU = mybir.ActivationFunctionType.Relu

P = 128
PACK = 4
MAX_TILES = 4
UNITS = [4] * 15 + [2, 2]
N_UNITS = len(UNITS)
VECTOR_WIDENS = {(4, 0), (9, 0)}
VECTOR_PARTS = {N_UNITS - 1: 2, N_UNITS - 2: 2, N_UNITS - 3: 3, N_UNITS - 4: 2, N_UNITS - 5: 1}
STARTS = [P * sum(UNITS[:c]) for c in range(N_UNITS)]
assert P * sum(UNITS) == ROWS


def tile_dpn_t_w4_kernel(tc, x_bytes, x_scale, W1_words, W1_scales, b1, W2_words, W2_scales, b2, out):
    nc = tc.nc

    with ExitStack() as ctx:
        keep = ctx.enter_context(tc.tile_pool(name="keep", bufs=1))
        work = ctx.enter_context(tc.tile_pool(name="work", bufs=3))
        psum = ctx.enter_context(tc.psum_pool(name="psum", bufs=1))

        ident = keep.tile([P, P], F32, name="ident")
        x_scales = keep.tile([P, PACK], F32, name="x_scales")
        w1_raw = keep.tile([P, HID * 2], U8, name="w1_raw", align_bytes=64)
        w1 = keep.tile([P, HID * 2], U8, name="w1", align_bytes=64)
        w1s_raw = keep.tile([P, HID], U8, name="w1s_raw", align_bytes=64)
        w1s = keep.tile([P, HID], U8, name="w1s", align_bytes=64)
        w2 = keep.tile([P, 2, OUT * 2], U8, name="w2", align_bytes=64)
        w2s = keep.tile([P, 2, OUT], U8, name="w2s", align_bytes=64)
        b1_col = keep.tile([P, PACK], BF16, name="b1_col")
        b2_row = keep.tile([P, OUT], BF16, name="b2_row")
        warm = keep.tile([P, 1], F32, name="warm")

        x8 = {}

        def load(c, lo=0, hi=MAX_TILES):
            tiles = UNITS[c]
            if lo == 0:
                x8[c] = work.tile([P, MAX_TILES * D_IN], U8, name="x8", bufs=N_UNITS, align_bytes=64)
            cols = slice(D_IN * lo, D_IN * min(hi, tiles))
            src = x_bytes[STARTS[c] : STARTS[c] + P * tiles, :].rearrange("(p j) k -> p (j k)", j=tiles)
            nc.sync.dma_start(out=x8[c][:, cols], in_=src[:, cols])

        nc.vector.memset(w1s_raw[:].bitcast(U32), 0)
        nc.vector.memset(w2s[:].rearrange("p g n -> p (g n)").bitcast(U32), 0)
        nc.vector.memset(warm[:], 0.0)
        nc.scalar.dma_start(out=x_scales[:], in_=x_scale.rearrange("o (p t) -> p (o t)", t=PACK))
        load(0, 0, 2)
        nc.sync.dma_start(out=w1_raw[:], in_=W1_words[0])
        for q in range(4):
            nc.sync.dma_start(
                out=w1s_raw[32 * q : 32 * q + 4, :].bitcast(I32), in_=W1_scales[0, 4 * q : 4 * q + 4, :].bitcast(I32)
            )
        load(0, 2, 4)
        nc.scalar.dma_start(out=b1_col[:], in_=b1.rearrange("(p t) -> p t", t=PACK))
        nc.scalar.activation(out=warm[:], in_=warm[:], func=RELU)
        make_identity(nc, ident[:])
        load(1)
        load(2)
        nc.sync.dma_start(out=w2[:], in_=W2_words.rearrange("g p n -> p g n"))
        for q in range(4):
            nc.sync.dma_start(
                out=w2s[32 * q : 32 * q + 4, :, :].bitcast(I32),
                in_=W2_scales.bitcast(I32)[:, 4 * q : 4 * q + 4, :].rearrange("g q n -> q g n"),
            )
        nc.sync.dma_start(out=b2_row[:], in_=b2.partition_broadcast(P))
        for c in range(3, N_UNITS):
            load(c)

        def permute_weights():
            nc.vector.tensor_copy(
                out=w1[:].rearrange("p (t m b) -> p t m b", t=PACK, b=2),
                in_=w1_raw[:].rearrange("p (m t b) -> p t m b", t=PACK, b=2),
            )
            nc.vector.tensor_copy(
                out=w1s[:].rearrange("p (t m) -> p t m", t=PACK),
                in_=w1s_raw[:].rearrange("p (m t) -> p t m", t=PACK),
            )

        xb, xt, xg, xq, xs = {}, {}, {}, {}, {}
        h, hs, hg, hq, hsc = {}, {}, {}, {}, {}
        acc, ob = {}, {}

        def live(c, half=0):
            return 0 <= c < N_UNITS and 2 * half < UNITS[c]

        def widen_x(c, lo=0, hi=MAX_TILES):
            if not live(c):
                return
            if lo == 0:
                xb[c] = work.tile([P, MAX_TILES * D_IN], BF16, name="xb", bufs=4, align_bytes=64)
            cols = slice(D_IN * lo, D_IN * min(hi, UNITS[c]))
            copy = nc.vector.tensor_copy if (c, lo) in VECTOR_WIDENS else nc.scalar.copy
            copy(out=xb[c][:, cols], in_=x8[c][:, cols].bitcast(FP8))

        def transpose_x(c, half):
            if not live(c, half):
                return
            words = xb[c][:].bitcast(F32)
            xt[c, half] = psum.tile([P, 2, 2, P], F32, name="xt", bufs=2)
            for j in range(2):
                w0 = (2 * half + j) * (D_IN // 2)
                for u in range(2):
                    nc.tensor.transpose(xt[c, half][:, u, j, :], words[:, w0 + u : w0 + D_IN // 2 : 2], ident[:])

        def scale_x(c, half):
            if not live(c, half):
                return
            if half == 0:
                xg[c] = work.tile([P, MAX_TILES * D_IN], BF16, name="xg", align_bytes=64)
            nc.vector.tensor_tensor(
                out=xg[c][:, 2 * D_IN * half : 2 * D_IN * (half + 1)].rearrange("p (n u e) -> p n u e", u=2, e=2),
                in0=xt[c, half][:]
                .rearrange("p u j n -> p (u j n)")
                .bitcast(BF16)
                .rearrange("p (u n e) -> p n u e", u=2, e=2),
                in1=x_scales[:].rearrange("p (u e) -> p u e", e=2).unsqueeze(1).to_broadcast([P, 2 * P, 2, 2]),
                op=MULT,
            )

        def quantize_x(c):
            if not live(c):
                return
            n = P * UNITS[c]
            xq[c] = work.tile([P, MAX_TILES * P], U32, name="xq", bufs=5, align_bytes=64)
            xs[c] = work.tile([P, MAX_TILES * P], U8, name="xs", bufs=5, align_bytes=64)
            nc.vector.quantize_mx(
                out=xq[c][:, :n].bitcast(FP8X4), scales=xs[c][:, :n], in_=xg[c][:, : PACK * n]
            )

        def layer1(c, t):
            if not live(c):
                return
            n = P * UNITS[c]
            h[c, t] = psum.tile([P, MAX_TILES * P], F32, name="h%d" % t)
            nc.tensor.matmul_mx(
                out=h[c, t][:, :n],
                lhsT=w1[:, 2 * P * t : 2 * P * (t + 1)].bitcast(FP4X4),
                lhsT_scale=w1s[:, P * t : P * (t + 1)],
                rhs=xq[c][:, :n].bitcast(FP8X4),
                rhs_scale=xs[c][:, :n],
                start=True,
                stop=True,
            )

        def relu(c, t):
            if not live(c):
                return
            n = P * UNITS[c]
            if c not in hs:
                hs[c] = work.tile([P, PACK, MAX_TILES * P], BF16, name="hs", align_bytes=64)
            dst = hs[c][:, t, :n]
            nc.scalar.activation(out=dst, in_=h[c, t][:, :n], func=RELU, bias=b1_col[:, t : t + 1])

        def interleave_h(c, on_vector=False):
            if not live(c):
                return
            if c not in hg:
                hg[c] = work.tile([P, MAX_TILES * P, PACK], BF16, name="hg", align_bytes=64)
            for j in range(UNITS[c]):
                if on_vector != (j < VECTOR_PARTS.get(c, 0)):
                    continue
                rows = slice(P * j, P * (j + 1))
                src = hs[c][:, :, rows].rearrange("p t n -> p n t")
                if on_vector:
                    nc.vector.tensor_copy(out=hg[c][:, rows, :], in_=src)
                else:
                    nc.gpsimd.tensor_scalar(
                        out=hg[c][:, rows, :], in0=src, scalar1=1.0, scalar2=0.0, op0=MULT, op1=ADD
                    )

        def quantize_h(c):
            if not live(c):
                return
            n = P * UNITS[c]
            hq[c] = work.tile([P, MAX_TILES * P], U32, name="hq", align_bytes=64)
            hsc[c] = work.tile([P, MAX_TILES * P], U8, name="hsc", align_bytes=64)
            nc.vector.quantize_mx(
                out=hq[c][:, :n].bitcast(FP8X4), scales=hsc[c][:, :n], in_=hg[c][:, :n, :].rearrange("p n t -> p (n t)")
            )

        def layer2(c):
            if not live(c):
                return
            acc[c] = psum.tile([P, MAX_TILES, OUT], F32, name="acc", bufs=2)
            for j in range(UNITS[c]):
                cols = slice(P * j, P * (j + 1))
                for g, codes, scales in ((0, xq[c], xs[c]), (1, hq[c], hsc[c])):
                    nc.tensor.matmul_mx(
                        out=acc[c][:, j, :],
                        lhsT=codes[:, cols].bitcast(FP8X4),
                        lhsT_scale=scales[:, cols],
                        rhs=w2[:, g, :].bitcast(FP4X4),
                        rhs_scale=w2s[:, g, :],
                        start=(g == 0),
                        stop=(g == 1),
                    )

        def add_b2(c):
            if not live(c):
                return
            tiles = UNITS[c]
            ob[c] = work.tile([P, MAX_TILES, OUT], F32, name="ob")
            nc.vector.tensor_tensor(
                out=ob[c][:, :tiles, :],
                in0=acc[c][:, :tiles, :],
                in1=b2_row[:].unsqueeze(1).to_broadcast([P, tiles, OUT]),
                op=ADD,
            )

        def store(c):
            if not live(c):
                return
            tiles = UNITS[c]
            nc.sync.dma_start(
                out=out[STARTS[c] : STARTS[c] + P * tiles, :].rearrange("(p j) o -> p (j o)", j=tiles),
                in_=ob[c][:, :tiles, :].rearrange("p j o -> p (j o)"),
            )

        with tc.manual_schedule():
            widen_x(0, 0, 2)
            permute_weights()
            widen_x(0, 2, 4)
            for s in range(-5, N_UNITS):
                for t in range(PACK):
                    relu(s + 2, t)
                widen_x(s + 6)
                if s == -5:
                    transpose_x(0, 0)
                    transpose_x(0, 1)
                quantize_h(s)
                interleave_h(s + 1)
                layer2(s)
                scale_x(s + 4, 0)
                scale_x(s + 4, 1)
                for t in range(PACK):
                    layer1(s + 3, t)
                interleave_h(s + 1, on_vector=True)
                add_b2(s)
                quantize_x(s + 4)
                if s > -5:
                    transpose_x(s + 5, 0)
                    transpose_x(s + 5, 1)
                store(s)
